import numpy as np
import ml_dtypes


def mxq(x, axis, fmt="e4m3"):
    dtype, down = {"e4m3": (ml_dtypes.float8_e4m3fn, 7), "e5m2": (ml_dtypes.float8_e5m2, 14)}[fmt]
    v = np.moveaxis(np.asarray(x, np.float32).astype(ml_dtypes.bfloat16).astype(np.float64), axis, -1)
    blocks = v.reshape(v.shape[:-1] + (-1, 32))
    amax = np.abs(blocks).max(-1, keepdims=True)
    byte = np.maximum(np.where(amax > 0, np.frexp(amax)[1] - 1 + 127, 0) - down, 1)
    scale = np.exp2(byte - 127.0)
    codes = (blocks / scale).astype(np.float32).astype(dtype).astype(np.float64)
    return np.moveaxis((codes * scale).reshape(v.shape), -1, axis)


WIDE = False


def mx_kscale(k):
    if not WIDE:
        return np.ones(k)
    levels = np.array([10, -10, 5, -5, 0])
    a = np.random.permutation(np.resize(levels, k // 512 * 4)).reshape(k // 512, 4)
    idx = np.arange(k)
    return np.exp2(a[idx // 512, idx % 128 // 32])


BF16 = ml_dtypes.bfloat16


def bf(x):
    return np.asarray(x, np.float32).astype(BF16)


def f64(x):
    return np.asarray(x).astype(np.float64)


B, L, S, D, DA, H, MLP = 2, 3, 256, 1024, 1024, 16, 4096
EPS = 1e-5


def layer_norm(u, g, b):
    mu = u.mean(-1, keepdims=True)
    var = ((u - mu) ** 2).mean(-1, keepdims=True)
    return (u - mu) / np.sqrt(var + EPS) * g + b


def grn(st, stq, W, b, g, be):
    w = np.maximum((stq @ mxq(f64(W), 0, "e4m3")).reshape(B, L, S, D) + f64(b), 0.0)
    n = layer_norm(st, f64(g), f64(be))
    return (w + n).sum(1)


def setup_inputs():
    s = mx_kscale(D)
    r = np.random.standard_normal
    return {"layer_outputs": bf(r((B, L, S, D)) * s),
            "grn_q_W": bf(r((D, D)) / np.sqrt(D) / s[:, None]), "grn_q_b": bf(r(D) * 0.2), "grn_q_g": bf(1.0 + 0.1 * r(D)), "grn_q_be": bf(r(D) * 0.1),
            "grn_k_W": bf(r((D, D)) / np.sqrt(D) / s[:, None]), "grn_k_b": bf(r(D) * 0.2), "grn_k_g": bf(1.0 + 0.1 * r(D)), "grn_k_be": bf(r(D) * 0.1),
            "grn_v_W": bf(r((D, D)) / np.sqrt(D) / s[:, None]), "grn_v_b": bf(r(D) * 0.2), "grn_v_g": bf(1.0 + 0.1 * r(D)), "grn_v_be": bf(r(D) * 0.1)}


def reference(layer_outputs, grn_q_W, grn_q_b, grn_q_g, grn_q_be, grn_k_W, grn_k_b, grn_k_g, grn_k_be, grn_v_W, grn_v_b, grn_v_g, grn_v_be):
    st = f64(layer_outputs)
    stq = mxq(st.reshape(B * L * S, D), 1, "e4m3")
    q = grn(st, stq, grn_q_W, grn_q_b, grn_q_g, grn_q_be)
    k = grn(st, stq, grn_k_W, grn_k_b, grn_k_g, grn_k_be)
    v = grn(st, stq, grn_v_W, grn_v_b, grn_v_g, grn_v_be)
    return q, k, v

@@ -1,0 +1,303 @@
+from contextlib import ExitStack
+
+import concourse.mybir as mybir
+from concourse.masks import make_identity
+
+F32 = mybir.dt.float32
+BF16 = mybir.dt.bfloat16
+U32 = mybir.dt.uint32
+U8 = mybir.dt.uint8
+FP8X4 = mybir.dt.float8_e4m3fn_x4
+ACT = mybir.ActivationFunctionType
+ALU = mybir.AluOpType
+
+P = 128
+PACK = 4
+K_PASS = P * PACK
+
+BATCH, LAYERS, SEQ, DIM = 2, 3, 256, 1024
+EPS = 1e-5
+PROJ = 3
+K_PASSES = DIM // K_PASS
+TOK = BATCH * SEQ
+TOK_TILES = TOK // P
+F_TILES = DIM // P
+GROUP = 4
+GROUP_F = GROUP * P
+GROUPS = PROJ * F_TILES // GROUP
+BANK = 512
+STATS = 6
+STATS_MAX = 512
+
+FLOPS = 2 * BATCH * LAYERS * SEQ * DIM * PROJ * DIM
+
+
+def tile_dcadecoderblock_pa_kernel(
+    tc,
+    layer_outputs,
+    grn_q_W, grn_q_b, grn_q_g, grn_q_be,
+    grn_k_W, grn_k_b, grn_k_g, grn_k_be,
+    grn_v_W, grn_v_b, grn_v_g, grn_v_be,
+    out_0, out_1, out_2,
+):
+    nc = tc.nc
+    weights = [grn_q_W, grn_k_W, grn_v_W]
+    outs = [out_0, out_1, out_2]
+    vectors = [grn_q_b, grn_k_b, grn_v_b, grn_q_g, grn_k_g, grn_v_g, grn_q_be, grn_k_be, grn_v_be]
+    n_ft = PROJ * F_TILES
+
+    with ExitStack() as ctx:
+        const = ctx.enter_context(tc.tile_pool(name="const", bufs=1))
+        x_stage = ctx.enter_context(tc.tile_pool(name="x_stage", bufs=2))
+        w_load = ctx.enter_context(tc.tile_pool(name="w_load", bufs=4))
+        w_stage = ctx.enter_context(tc.tile_pool(name="w_stage", bufs=2))
+        w_keep = ctx.enter_context(tc.tile_pool(name="w_keep", bufs=3))
+        sums = ctx.enter_context(tc.tile_pool(name="sums", bufs=16))
+        rows_pool = ctx.enter_context(tc.tile_pool(name="rows", bufs=4))
+        psum_acc = ctx.enter_context(tc.psum_pool(name="psum_acc", bufs=5))
+        psum_tp = ctx.enter_context(tc.psum_pool(name="psum_tp", bufs=3))
+
+        ident_f32 = const.tile([P, P], F32)
+        make_identity(nc, ident_f32[:])
+        ident_bf16 = const.tile([P, P], BF16)
+        make_identity(nc, ident_bf16[:])
+        eps = const.tile([P, 1], F32)
+        nc.vector.memset(eps[:], EPS)
+        table_warm = const.tile([P, 1], F32)
+        nc.scalar.activation(out=table_warm[:], in_=eps[:], func=ACT.Sqrt)
+
+        x_sb = const.tile([P, LAYERS * TOK_TILES, DIM], BF16)
+
+        def load_layer(l):
+            for b in range(BATCH):
+                rt = l * TOK_TILES + 2 * b
+                nc.sync.dma_start(
+                    out=x_sb[:, rt : rt + 2, :],
+                    in_=layer_outputs[b, l, :, :].rearrange("(h p) d -> p h d", p=P),
+                )
+
+        w_raw = {}
+
+        def load_weights(n):
+            t, half = divmod(n, 2)
+            w_raw[n] = w_load.tile([P, K_PASSES, PACK, GROUP_F], BF16, name="w_raw")
+            for g in range(K_PASSES):
+                for u in range(2):
+                    k0 = g * K_PASS + u * 2 * P
+                    nc.sync.dma_start(
+                        out=w_raw[n][:, g, 2 * u : 2 * u + 2, :],
+                        in_=weights[t][k0 : k0 + 2 * P, half * GROUP_F : (half + 1) * GROUP_F].rearrange(
+                            "(p e) c -> p e c", e=2
+                        ),
+                    )
+
+        vec_rows = const.tile([P, P], BF16)
+        nc.vector.memset(vec_rows[:], 0.0)
+        for v, vec in enumerate(vectors):
+            nc.scalar.dma_start(
+                out=vec_rows[v * F_TILES : (v + 1) * F_TILES, :],
+                in_=vec.rearrange("(r c) -> r c", c=P),
+            )
+
+        load_layer(0)
+        load_weights(0)
+        load_layer(1)
+        load_layer(2)
+        load_weights(1)
+        load_weights(2)
+        load_weights(3)
+
+        x_codes = const.tile([P, LAYERS * K_PASSES * TOK], U32, align_bytes=64)
+        x_scales = const.tile([P, LAYERS * K_PASSES * TOK], U8, align_bytes=64)
+
+        def quantise_layer(l):
+            grouped = x_stage.tile([P, K_PASSES * TOK * PACK], BF16, align_bytes=64)
+            grouped_words = grouped[:].bitcast(F32).rearrange("p (g r u) -> p g r u", g=K_PASSES, u=2)
+            for j in range(TOK_TILES):
+                x_words = x_sb[:, l * TOK_TILES + j, :].bitcast(F32)
+                xt = psum_tp.tile([P, BANK], F32, tag="tp")
+                for gu in range(BANK // P):
+                    nc.tensor.transpose(xt[:, gu * P : (gu + 1) * P], x_words[:, gu * P : (gu + 1) * P], ident_f32[:])
+                nc.scalar.copy(
+                    out=grouped_words[:, :, j * P : (j + 1) * P, :],
+                    in_=xt[:].rearrange("p (g u r) -> p g r u", g=K_PASSES, u=2),
+                )
+            cols = slice(l * K_PASSES * TOK, (l + 1) * K_PASSES * TOK)
+            nc.vector.quantize_mx(out=x_codes[:, cols].bitcast(FP8X4), scales=x_scales[:, cols], in_=grouped[:])
+
+        w_grouped = {}
+        w_codes = {}
+        w_scales = {}
+
+        def regroup_weights(n):
+            w_grouped[n] = w_stage.tile([P, K_PASSES, GROUP_F, PACK], BF16, align_bytes=64, name="w_grouped")
+            for g in range(K_PASSES):
+                dst = w_grouped[n][:, g, :, :].rearrange("p (c i) t -> p c t i", i=4)
+                src = w_raw[n][:, g, :, :].rearrange("p t (c i) -> p c t i", i=4)
+                if g == 0:
+                    nc.vector.tensor_copy(out=dst, in_=src)
+                else:
+                    nc.scalar.copy(out=dst, in_=src)
+
+        def quantise_weights(n):
+            w_codes[n] = w_keep.tile([P, K_PASSES * GROUP_F], U32, align_bytes=64, name="w_codes")
+            w_scales[n] = w_keep.tile([P, K_PASSES * GROUP_F], U8, align_bytes=64, name="w_scales")
+            nc.vector.quantize_mx(
+                out=w_codes[n][:].bitcast(FP8X4),
+                scales=w_scales[n][:],
+                in_=w_grouped[n][:].rearrange("p g c t -> p (g c t)"),
+            )
+
+        params = const.tile([P, P], F32)
+        neg_bias = const.tile([P, n_ft], F32)
+        shift3 = const.tile([P, n_ft], F32)
+        const_term = const.tile([P, n_ft], F32)
+
+        def spread_vectors():
+            vec_cols = psum_tp.tile([P, P], BF16, tag="tp")
+            nc.tensor.transpose(vec_cols[:], vec_rows[:], ident_bf16[:])
+            nc.vector.tensor_copy(out=params[:], in_=vec_cols[:])
+            bias = params[:, 0:n_ft]
+            shift = params[:, 2 * n_ft : 3 * n_ft]
+            nc.vector.tensor_scalar_mul(out=neg_bias[:], in0=bias, scalar1=-1.0)
+            nc.vector.tensor_scalar_mul(out=shift3[:], in0=shift, scalar1=float(LAYERS))
+            nc.vector.scalar_tensor_tensor(
+                out=const_term[:], in0=bias, scalar=float(LAYERS - 1), in1=shift3[:], op0=ALU.mult, op1=ALU.add
+            )
+
+        relu_sum = {}
+
+        def project_group(n):
+            for l in range(LAYERS):
+                for i in range(GROUP):
+                    ft = n * GROUP + i
+                    acc = psum_acc.tile([P, TOK], F32, tag="acc")
+                    for g in range(K_PASSES):
+                        w_cols = slice(g * GROUP_F + i * P, g * GROUP_F + (i + 1) * P)
+                        x_cols = slice((l * K_PASSES + g) * TOK, (l * K_PASSES + g + 1) * TOK)
+                        nc.tensor.matmul_mx(
+                            out=acc[:],
+                            lhsT=w_codes[n][:, w_cols].bitcast(FP8X4),
+                            lhsT_scale=w_scales[n][:, w_cols],
+                            rhs=x_codes[:, x_cols].bitcast(FP8X4),
+                            rhs_scale=x_scales[:, x_cols],
+                            start=(g == 0),
+                            stop=(g == K_PASSES - 1),
+                        )
+                    if l == 0:
+                        relu_sum[ft] = sums.tile([P, TOK], F32, name="relu_sum")
+                        nc.scalar.activation(
+                            out=relu_sum[ft][:], in_=acc[:], func=ACT.Relu, bias=params[:, ft : ft + 1], scale=1.0
+                        )
+                    else:
+                        nc.vector.scalar_tensor_tensor(
+                            out=relu_sum[ft][:],
+                            in0=acc[:],
+                            scalar=neg_bias[:, ft : ft + 1],
+                            in1=relu_sum[ft][:],
+                            op0=ALU.max,
+                            op1=ALU.add,
+                        )
+
+        n_rt = LAYERS * TOK_TILES
+        chunks = DIM // STATS_MAX
+        stats = const.tile([P, n_rt, chunks, STATS], F32)
+        mean_var = const.tile([P, n_rt, 2], F32)
+        std = const.tile([P, n_rt], F32)
+        rstd = const.tile([P, n_rt], F32)
+        mean_rstd = const.tile([P, n_rt], F32)
+        mean_rstd01 = const.tile([P, TOK_TILES], F32)
+        neg_mean_sum = const.tile([P, TOK_TILES], F32)
+        z = const.tile([P, TOK_TILES, DIM], F32)
+        ln_term = {}
+
+        def layer_statistics(l):
+            for j in range(TOK_TILES):
+                rt = l * TOK_TILES + j
+                for c in range(chunks):
+                    nc.vector.bn_stats(out=stats[:, rt, c, :], in_=x_sb[:, rt, c * STATS_MAX : (c + 1) * STATS_MAX])
+                nc.vector.bn_aggr(out=mean_var[:, rt, :], in_=stats[:, rt, :, :].rearrange("p c s -> p (c s)"))
+
+        def norm_scalars():
+            nc.scalar.activation(out=std[:], in_=mean_var[:, :, 1], func=ACT.Sqrt, bias=eps[:, 0:1], scale=1.0)
+            nc.vector.reciprocal(out=rstd[:], in_=std[:])
+            nc.vector.tensor_mul(out=mean_rstd[:], in0=mean_var[:, :, 0], in1=rstd[:])
+            nc.vector.tensor_add(
+                out=mean_rstd01[:], in0=mean_rstd[:, 0:TOK_TILES], in1=mean_rstd[:, TOK_TILES : 2 * TOK_TILES]
+            )
+            nc.vector.scalar_tensor_tensor(
+                out=neg_mean_sum[:],
+                in0=mean_rstd01[:],
+                scalar=-1.0,
+                in1=mean_rstd[:, 2 * TOK_TILES : 3 * TOK_TILES],
+                op0=ALU.mult,
+                op1=ALU.subtract,
+            )
+
+        def normalised_sum(j):
+            nc.scalar.activation(
+                out=z[:, j, :], in_=x_sb[:, j, :], func=ACT.Identity,
+                scale=rstd[:, j : j + 1], bias=neg_mean_sum[:, j : j + 1],
+            )
+            for l in range(1, LAYERS):
+                rt = l * TOK_TILES + j
+                nc.vector.scalar_tensor_tensor(
+                    out=z[:, j, :], in0=x_sb[:, rt, :], scalar=rstd[:, rt : rt + 1], in1=z[:, j, :],
+                    op0=ALU.mult, op1=ALU.add,
+                )
+
+        def norm_terms(f):
+            zt = psum_tp.tile([P, BANK], F32, tag="tp")
+            for j in range(TOK_TILES):
+                nc.tensor.transpose(zt[:, j * P : (j + 1) * P], z[:, j, f * P : (f + 1) * P], ident_f32[:])
+            for t in range(PROJ):
+                ft = t * F_TILES + f
+                ln_term[ft] = const.tile([P, TOK], F32, name="ln_term%d" % ft)
+                nc.scalar.activation(
+                    out=ln_term[ft][:], in_=zt[:], func=ACT.Identity,
+                    scale=params[:, n_ft + ft : n_ft + ft + 1], bias=const_term[:, ft : ft + 1],
+                )
+
+        def finish_group(n):
+            t, half = divmod(n, 2)
+            for i in range(GROUP):
+                ft = n * GROUP + i
+                nc.gpsimd.tensor_tensor(out=ln_term[ft][:], in0=ln_term[ft][:], in1=relu_sum[ft][:], op=ALU.add)
+            for j in range(TOK_TILES):
+                b, h = divmod(j, 2)
+                back = psum_tp.tile([P, BANK], F32, tag="tp")
+                for i in range(GROUP):
+                    nc.tensor.transpose(
+                        back[:, i * P : (i + 1) * P], ln_term[n * GROUP + i][:, j * P : (j + 1) * P], ident_f32[:]
+                    )
+                rows = rows_pool.tile([P, GROUP_F], F32)
+                nc.scalar.copy(out=rows[:], in_=back[:])
+                nc.sync.dma_start(
+                    out=outs[t][b, h * P : (h + 1) * P, half * GROUP_F : (half + 1) * GROUP_F], in_=rows[:]
+                )
+
+        quantise_layer(0)
+        regroup_weights(0)
+        quantise_weights(0)
+        spread_vectors()
+        quantise_layer(1)
+        quantise_layer(2)
+        regroup_weights(1)
+        quantise_weights(1)
+        project_group(0)
+        for l in range(LAYERS):
+            layer_statistics(l)
+        norm_scalars()
+        for j in range(TOK_TILES):
+            normalised_sum(j)
+        for f in range(F_TILES):
+            norm_terms(f)
+        for n in range(1, GROUPS):
+            if n + 3 < GROUPS:
+                load_weights(n + 3)
+            if n + 1 < GROUPS:
+                regroup_weights(n + 1)
+                quantise_weights(n + 1)
+            project_group(n)
+            finish_group(n - 1)
+        finish_group(GROUPS - 1)

@@ -49,10 +49,11 @@ def tile_dcadecoderblock_pa_kernel(
     with ExitStack() as ctx:
         const = ctx.enter_context(tc.tile_pool(name="const", bufs=1))
         x_stage = ctx.enter_context(tc.tile_pool(name="x_stage", bufs=2))
-        w_load = ctx.enter_context(tc.tile_pool(name="w_load", bufs=4))
+        w_load = ctx.enter_context(tc.tile_pool(name="w_load", bufs=3))
         w_stage = ctx.enter_context(tc.tile_pool(name="w_stage", bufs=2))
         w_keep = ctx.enter_context(tc.tile_pool(name="w_keep", bufs=3))
-        sums = ctx.enter_context(tc.tile_pool(name="sums", bufs=16))
+        norm_pool = ctx.enter_context(tc.tile_pool(name="norm", bufs=36))
+        sums = ctx.enter_context(tc.tile_pool(name="sums", bufs=14))
         rows_pool = ctx.enter_context(tc.tile_pool(name="rows", bufs=4))
         psum_acc = ctx.enter_context(tc.psum_pool(name="psum_acc", bufs=5))
         psum_tp = ctx.enter_context(tc.psum_pool(name="psum_tp", bufs=3))
@@ -105,7 +106,6 @@ def tile_dcadecoderblock_pa_kernel(
         load_layer(2)
         load_weights(1)
         load_weights(2)
-        load_weights(3)
 
         x_codes = const.tile([P, LAYERS * K_PASSES * TOK], U32, align_bytes=64)
         x_scales = const.tile([P, LAYERS * K_PASSES * TOK], U8, align_bytes=64)
@@ -167,37 +167,36 @@ def tile_dcadecoderblock_pa_kernel(
 
         relu_sum = {}
 
-        def project_group(n):
-            for l in range(LAYERS):
-                for i in range(GROUP):
-                    ft = n * GROUP + i
-                    acc = psum_acc.tile([P, TOK], F32, tag="acc")
-                    for g in range(K_PASSES):
-                        w_cols = slice(g * GROUP_F + i * P, g * GROUP_F + (i + 1) * P)
-                        x_cols = slice((l * K_PASSES + g) * TOK, (l * K_PASSES + g + 1) * TOK)
-                        nc.tensor.matmul_mx(
-                            out=acc[:],
-                            lhsT=w_codes[n][:, w_cols].bitcast(FP8X4),
-                            lhsT_scale=w_scales[n][:, w_cols],
-                            rhs=x_codes[:, x_cols].bitcast(FP8X4),
-                            rhs_scale=x_scales[:, x_cols],
-                            start=(g == 0),
-                            stop=(g == K_PASSES - 1),
-                        )
-                    if l == 0:
-                        relu_sum[ft] = sums.tile([P, TOK], F32, name="relu_sum")
-                        nc.scalar.activation(
-                            out=relu_sum[ft][:], in_=acc[:], func=ACT.Relu, bias=params[:, ft : ft + 1], scale=1.0
-                        )
-                    else:
-                        nc.vector.scalar_tensor_tensor(
-                            out=relu_sum[ft][:],
-                            in0=acc[:],
-                            scalar=neg_bias[:, ft : ft + 1],
-                            in1=relu_sum[ft][:],
-                            op0=ALU.max,
-                            op1=ALU.add,
-                        )
+        def project(n, l):
+            for i in range(GROUP):
+                ft = n * GROUP + i
+                acc = psum_acc.tile([P, TOK], F32, tag="acc")
+                for g in range(K_PASSES):
+                    w_cols = slice(g * GROUP_F + i * P, g * GROUP_F + (i + 1) * P)
+                    x_cols = slice((l * K_PASSES + g) * TOK, (l * K_PASSES + g + 1) * TOK)
+                    nc.tensor.matmul_mx(
+                        out=acc[:],
+                        lhsT=w_codes[n][:, w_cols].bitcast(FP8X4),
+                        lhsT_scale=w_scales[n][:, w_cols],
+                        rhs=x_codes[:, x_cols].bitcast(FP8X4),
+                        rhs_scale=x_scales[:, x_cols],
+                        start=(g == 0),
+                        stop=(g == K_PASSES - 1),
+                    )
+                if l == 0:
+                    relu_sum[ft] = sums.tile([P, TOK], F32, name="relu_sum")
+                    nc.scalar.activation(
+                        out=relu_sum[ft][:], in_=acc[:], func=ACT.Relu, bias=params[:, ft : ft + 1], scale=1.0
+                    )
+                else:
+                    nc.vector.scalar_tensor_tensor(
+                        out=relu_sum[ft][:],
+                        in0=acc[:],
+                        scalar=neg_bias[:, ft : ft + 1],
+                        in1=relu_sum[ft][:],
+                        op0=ALU.max,
+                        op1=ALU.add,
+                    )
 
         n_rt = LAYERS * TOK_TILES
         chunks = DIM // STATS_MAX
@@ -205,10 +204,8 @@ def tile_dcadecoderblock_pa_kernel(
         mean_var = const.tile([P, n_rt, 2], F32)
         std = const.tile([P, n_rt], F32)
         rstd = const.tile([P, n_rt], F32)
-        mean_rstd = const.tile([P, n_rt], F32)
-        mean_rstd01 = const.tile([P, TOK_TILES], F32)
-        neg_mean_sum = const.tile([P, TOK_TILES], F32)
-        z = const.tile([P, TOK_TILES, DIM], F32)
+        neg_mean = const.tile([P, n_rt], F32)
+        z_part = {}
         ln_term = {}
 
         def layer_statistics(l):
@@ -217,42 +214,42 @@ def tile_dcadecoderblock_pa_kernel(
                 for c in range(chunks):
                     nc.vector.bn_stats(out=stats[:, rt, c, :], in_=x_sb[:, rt, c * STATS_MAX : (c + 1) * STATS_MAX])
                 nc.vector.bn_aggr(out=mean_var[:, rt, :], in_=stats[:, rt, :, :].rearrange("p c s -> p (c s)"))
+            rts = slice(l * TOK_TILES, (l + 1) * TOK_TILES)
+            nc.scalar.activation(out=std[:, rts], in_=mean_var[:, rts, 1], func=ACT.Sqrt, bias=eps[:, 0:1], scale=1.0)
+            nc.vector.tensor_scalar_mul(out=neg_mean[:, rts], in0=mean_var[:, rts, 0], scalar1=-1.0)
+            nc.vector.reciprocal(out=rstd[:, rts], in_=std[:, rts])
 
-        def norm_scalars():
-            nc.scalar.activation(out=std[:], in_=mean_var[:, :, 1], func=ACT.Sqrt, bias=eps[:, 0:1], scale=1.0)
-            nc.vector.reciprocal(out=rstd[:], in_=std[:])
-            nc.vector.tensor_mul(out=mean_rstd[:], in0=mean_var[:, :, 0], in1=rstd[:])
-            nc.vector.tensor_add(
-                out=mean_rstd01[:], in0=mean_rstd[:, 0:TOK_TILES], in1=mean_rstd[:, TOK_TILES : 2 * TOK_TILES]
-            )
-            nc.vector.scalar_tensor_tensor(
-                out=neg_mean_sum[:],
-                in0=mean_rstd01[:],
-                scalar=-1.0,
-                in1=mean_rstd[:, 2 * TOK_TILES : 3 * TOK_TILES],
-                op0=ALU.mult,
-                op1=ALU.subtract,
-            )
-
-        def normalised_sum(j):
-            nc.scalar.activation(
-                out=z[:, j, :], in_=x_sb[:, j, :], func=ACT.Identity,
-                scale=rstd[:, j : j + 1], bias=neg_mean_sum[:, j : j + 1],
-            )
-            for l in range(1, LAYERS):
-                rt = l * TOK_TILES + j
-                nc.vector.scalar_tensor_tensor(
-                    out=z[:, j, :], in0=x_sb[:, rt, :], scalar=rstd[:, rt : rt + 1], in1=z[:, j, :],
-                    op0=ALU.mult, op1=ALU.add,
-                )
+        def normalised_parts(l):
+            for half in range(DIM // BANK):
+                for j in range(TOK_TILES):
+                    rt = l * TOK_TILES + j
+                    z_part[l, j, half] = norm_pool.tile([P, BANK], F32, name="z_part", tag="norm")
+                    nc.gpsimd.tensor_scalar(
+                        out=z_part[l, j, half][:],
+                        in0=x_sb[:, rt, half * BANK : (half + 1) * BANK],
+                        scalar1=neg_mean[:, rt : rt + 1],
+                        scalar2=rstd[:, rt : rt + 1],
+                        op0=ALU.add,
+                        op1=ALU.mult,
+                    )
 
         def norm_terms(f):
+            half, f_in_half = divmod(f, BANK // P)
+            f_cols = slice(f_in_half * P, (f_in_half + 1) * P)
             zt = psum_tp.tile([P, BANK], F32, tag="tp")
             for j in range(TOK_TILES):
-                nc.tensor.transpose(zt[:, j * P : (j + 1) * P], z[:, j, f * P : (f + 1) * P], ident_f32[:])
+                for l in range(LAYERS):
+                    nc.tensor.matmul(
+                        out=zt[:, j * P : (j + 1) * P],
+                        lhsT=z_part[l, j, half][:, f_cols],
+                        rhs=ident_f32[:],
+                        is_transpose=True,
+                        start=(l == 0),
+                        stop=(l == LAYERS - 1),
+                    )
             for t in range(PROJ):
                 ft = t * F_TILES + f
-                ln_term[ft] = const.tile([P, TOK], F32, name="ln_term%d" % ft)
+                ln_term[ft] = norm_pool.tile([P, TOK], F32, name="ln_term", tag="norm")
                 nc.scalar.activation(
                     out=ln_term[ft][:], in_=zt[:], func=ACT.Identity,
                     scale=params[:, n_ft + ft : n_ft + ft + 1], bias=const_term[:, ft : ft + 1],
@@ -271,7 +268,7 @@ def tile_dcadecoderblock_pa_kernel(
                         back[:, i * P : (i + 1) * P], ln_term[n * GROUP + i][:, j * P : (j + 1) * P], ident_f32[:]
                     )
                 rows = rows_pool.tile([P, GROUP_F], F32)
-                nc.scalar.copy(out=rows[:], in_=back[:])
+                nc.any.tensor_copy(out=rows[:], in_=back[:])
                 nc.sync.dma_start(
                     out=outs[t][b, h * P : (h + 1) * P, half * GROUP_F : (half + 1) * GROUP_F], in_=rows[:]
                 )
@@ -281,23 +278,27 @@ def tile_dcadecoderblock_pa_kernel(
         quantise_weights(0)
         spread_vectors()
         quantise_layer(1)
+        project(0, 0)
+        layer_statistics(0)
+        normalised_parts(0)
         quantise_layer(2)
+        project(0, 1)
+        layer_statistics(1)
+        normalised_parts(1)
         regroup_weights(1)
         quantise_weights(1)
-        project_group(0)
-        for l in range(LAYERS):
-            layer_statistics(l)
-        norm_scalars()
-        for j in range(TOK_TILES):
-            normalised_sum(j)
+        project(0, 2)
+        layer_statistics(2)
+        normalised_parts(2)
         for f in range(F_TILES):
             norm_terms(f)
         for n in range(1, GROUPS):
-            if n + 3 < GROUPS:
-                load_weights(n + 3)
+            if n + 2 < GROUPS:
+                load_weights(n + 2)
             if n + 1 < GROUPS:
                 regroup_weights(n + 1)
                 quantise_weights(n + 1)
-            project_group(n)
+            for l in range(LAYERS):
+                project(n, l)
             finish_group(n - 1)
         finish_group(GROUPS - 1)

@@ -24,7 +24,8 @@ TOK_TILES = TOK // P
 F_TILES = DIM // P
 GROUP = 4
 GROUP_F = GROUP * P
-GROUPS = PROJ * F_TILES // GROUP
+HALVES = F_TILES // GROUP
+GROUPS = PROJ * HALVES
 BANK = 512
 STATS = 6
 STATS_MAX = 512
@@ -46,6 +47,10 @@ def tile_dcadecoderblock_pa_kernel(
     vectors = [grn_q_b, grn_k_b, grn_v_b, grn_q_g, grn_k_g, grn_v_g, grn_q_be, grn_k_be, grn_v_be]
     n_ft = PROJ * F_TILES
 
+    def feature_tile(n, i):
+        half, t = divmod(n, PROJ)
+        return t * F_TILES + half * GROUP + i
+
     with ExitStack() as ctx:
         const = ctx.enter_context(tc.tile_pool(name="const", bufs=1))
         x_stage = ctx.enter_context(tc.tile_pool(name="x_stage", bufs=2))
@@ -55,8 +60,8 @@ def tile_dcadecoderblock_pa_kernel(
         norm_pool = ctx.enter_context(tc.tile_pool(name="norm", bufs=36))
         sums = ctx.enter_context(tc.tile_pool(name="sums", bufs=14))
         rows_pool = ctx.enter_context(tc.tile_pool(name="rows", bufs=4))
-        psum_acc = ctx.enter_context(tc.psum_pool(name="psum_acc", bufs=5))
-        psum_tp = ctx.enter_context(tc.psum_pool(name="psum_tp", bufs=3))
+        psum_acc = ctx.enter_context(tc.psum_pool(name="psum_acc", bufs=4))
+        psum_tp = ctx.enter_context(tc.psum_pool(name="psum_tp", bufs=4))
 
         ident_f32 = const.tile([P, P], F32)
         make_identity(nc, ident_f32[:])
@@ -80,7 +85,7 @@ def tile_dcadecoderblock_pa_kernel(
         w_raw = {}
 
         def load_weights(n):
-            t, half = divmod(n, 2)
+            half, t = divmod(n, PROJ)
             w_raw[n] = w_load.tile([P, K_PASSES, PACK, GROUP_F], BF16, name="w_raw")
             for g in range(K_PASSES):
                 for u in range(2):
@@ -134,10 +139,10 @@ def tile_dcadecoderblock_pa_kernel(
             for g in range(K_PASSES):
                 dst = w_grouped[n][:, g, :, :].rearrange("p (c i) t -> p c t i", i=4)
                 src = w_raw[n][:, g, :, :].rearrange("p t (c i) -> p c t i", i=4)
-                if g == 0:
-                    nc.vector.tensor_copy(out=dst, in_=src)
-                else:
+                if n < PROJ:
                     nc.scalar.copy(out=dst, in_=src)
+                else:
+                    nc.vector.tensor_copy(out=dst, in_=src)
 
         def quantise_weights(n):
             w_codes[n] = w_keep.tile([P, K_PASSES * GROUP_F], U32, align_bytes=64, name="w_codes")
@@ -169,7 +174,7 @@ def tile_dcadecoderblock_pa_kernel(
 
         def project(n, l):
             for i in range(GROUP):
-                ft = n * GROUP + i
+                ft = feature_tile(n, i)
                 acc = psum_acc.tile([P, TOK], F32, tag="acc")
                 for g in range(K_PASSES):
                     w_cols = slice(g * GROUP_F + i * P, g * GROUP_F + (i + 1) * P)
@@ -219,33 +224,32 @@ def tile_dcadecoderblock_pa_kernel(
             nc.vector.tensor_scalar_mul(out=neg_mean[:, rts], in0=mean_var[:, rts, 0], scalar1=-1.0)
             nc.vector.reciprocal(out=rstd[:, rts], in_=std[:, rts])
 
-        def normalised_parts(l):
-            for half in range(DIM // BANK):
-                for j in range(TOK_TILES):
-                    rt = l * TOK_TILES + j
-                    z_part[l, j, half] = norm_pool.tile([P, BANK], F32, name="z_part", tag="norm")
-                    nc.gpsimd.tensor_scalar(
-                        out=z_part[l, j, half][:],
-                        in0=x_sb[:, rt, half * BANK : (half + 1) * BANK],
-                        scalar1=neg_mean[:, rt : rt + 1],
-                        scalar2=rstd[:, rt : rt + 1],
-                        op0=ALU.add,
-                        op1=ALU.mult,
-                    )
+        def normalised_parts(l, half):
+            for j in range(TOK_TILES):
+                rt = l * TOK_TILES + j
+                z_part[l, j, half] = norm_pool.tile([P, BANK], F32, name="z_part", tag="norm")
+                nc.gpsimd.tensor_scalar(
+                    out=z_part[l, j, half][:],
+                    in0=x_sb[:, rt, half * BANK : (half + 1) * BANK],
+                    scalar1=neg_mean[:, rt : rt + 1],
+                    scalar2=rstd[:, rt : rt + 1],
+                    op0=ALU.add,
+                    op1=ALU.mult,
+                )
 
         def norm_terms(f):
             half, f_in_half = divmod(f, BANK // P)
             f_cols = slice(f_in_half * P, (f_in_half + 1) * P)
             zt = psum_tp.tile([P, BANK], F32, tag="tp")
             for j in range(TOK_TILES):
-                for l in range(LAYERS):
+                for l in reversed(range(LAYERS)):
                     nc.tensor.matmul(
                         out=zt[:, j * P : (j + 1) * P],
                         lhsT=z_part[l, j, half][:, f_cols],
                         rhs=ident_f32[:],
                         is_transpose=True,
-                        start=(l == 0),
-                        stop=(l == LAYERS - 1),
+                        start=(l == LAYERS - 1),
+                        stop=(l == 0),
                     )
             for t in range(PROJ):
                 ft = t * F_TILES + f
@@ -256,16 +260,17 @@ def tile_dcadecoderblock_pa_kernel(
                 )
 
         def finish_group(n):
-            t, half = divmod(n, 2)
+            half, t = divmod(n, PROJ)
+            adder = nc.vector if n == GROUPS - 1 else nc.gpsimd
             for i in range(GROUP):
-                ft = n * GROUP + i
-                nc.gpsimd.tensor_tensor(out=ln_term[ft][:], in0=ln_term[ft][:], in1=relu_sum[ft][:], op=ALU.add)
+                ft = feature_tile(n, i)
+                adder.tensor_tensor(out=ln_term[ft][:], in0=ln_term[ft][:], in1=relu_sum[ft][:], op=ALU.add)
             for j in range(TOK_TILES):
                 b, h = divmod(j, 2)
                 back = psum_tp.tile([P, BANK], F32, tag="tp")
                 for i in range(GROUP):
                     nc.tensor.transpose(
-                        back[:, i * P : (i + 1) * P], ln_term[n * GROUP + i][:, j * P : (j + 1) * P], ident_f32[:]
+                        back[:, i * P : (i + 1) * P], ln_term[feature_tile(n, i)][:, j * P : (j + 1) * P], ident_f32[:]
                     )
                 rows = rows_pool.tile([P, GROUP_F], F32)
                 nc.any.tensor_copy(out=rows[:], in_=back[:])
@@ -280,25 +285,29 @@ def tile_dcadecoderblock_pa_kernel(
         quantise_layer(1)
         project(0, 0)
         layer_statistics(0)
-        normalised_parts(0)
+        normalised_parts(0, 0)
         quantise_layer(2)
         project(0, 1)
         layer_statistics(1)
-        normalised_parts(1)
+        normalised_parts(1, 0)
         regroup_weights(1)
         quantise_weights(1)
         project(0, 2)
         layer_statistics(2)
-        normalised_parts(2)
-        for f in range(F_TILES):
-            norm_terms(f)
+        normalised_parts(2, 0)
+        for l in range(LAYERS):
+            normalised_parts(l, 1)
         for n in range(1, GROUPS):
             if n + 2 < GROUPS:
                 load_weights(n + 2)
             if n + 1 < GROUPS:
                 regroup_weights(n + 1)
                 quantise_weights(n + 1)
+            half_due, odd = divmod(n, 2)
             for l in range(LAYERS):
                 project(n, l)
+                if odd and half_due < HALVES and l < GROUP // 2:
+                    norm_terms(half_due * GROUP + 2 * l)
+                    norm_terms(half_due * GROUP + 2 * l + 1)
             finish_group(n - 1)
         finish_group(GROUPS - 1)

@@ -24,8 +24,7 @@ TOK_TILES = TOK // P
 F_TILES = DIM // P
 GROUP = 4
 GROUP_F = GROUP * P
-HALVES = F_TILES // GROUP
-GROUPS = PROJ * HALVES
+GROUPS = PROJ * F_TILES // GROUP
 BANK = 512
 STATS = 6
 STATS_MAX = 512
@@ -47,10 +46,6 @@ def tile_dcadecoderblock_pa_kernel(
     vectors = [grn_q_b, grn_k_b, grn_v_b, grn_q_g, grn_k_g, grn_v_g, grn_q_be, grn_k_be, grn_v_be]
     n_ft = PROJ * F_TILES
 
-    def feature_tile(n, i):
-        half, t = divmod(n, PROJ)
-        return t * F_TILES + half * GROUP + i
-
     with ExitStack() as ctx:
         const = ctx.enter_context(tc.tile_pool(name="const", bufs=1))
         x_stage = ctx.enter_context(tc.tile_pool(name="x_stage", bufs=2))
@@ -60,8 +55,8 @@ def tile_dcadecoderblock_pa_kernel(
         norm_pool = ctx.enter_context(tc.tile_pool(name="norm", bufs=36))
         sums = ctx.enter_context(tc.tile_pool(name="sums", bufs=14))
         rows_pool = ctx.enter_context(tc.tile_pool(name="rows", bufs=4))
-        psum_acc = ctx.enter_context(tc.psum_pool(name="psum_acc", bufs=4))
-        psum_tp = ctx.enter_context(tc.psum_pool(name="psum_tp", bufs=4))
+        psum_acc = ctx.enter_context(tc.psum_pool(name="psum_acc", bufs=5))
+        psum_tp = ctx.enter_context(tc.psum_pool(name="psum_tp", bufs=3))
 
         ident_f32 = const.tile([P, P], F32)
         make_identity(nc, ident_f32[:])
@@ -85,7 +80,7 @@ def tile_dcadecoderblock_pa_kernel(
         w_raw = {}
 
         def load_weights(n):
-            half, t = divmod(n, PROJ)
+            t, half = divmod(n, 2)
             w_raw[n] = w_load.tile([P, K_PASSES, PACK, GROUP_F], BF16, name="w_raw")
             for g in range(K_PASSES):
                 for u in range(2):
@@ -139,10 +134,10 @@ def tile_dcadecoderblock_pa_kernel(
             for g in range(K_PASSES):
                 dst = w_grouped[n][:, g, :, :].rearrange("p (c i) t -> p c t i", i=4)
                 src = w_raw[n][:, g, :, :].rearrange("p t (c i) -> p c t i", i=4)
-                if n < PROJ:
-                    nc.scalar.copy(out=dst, in_=src)
-                else:
+                if g == 0:
                     nc.vector.tensor_copy(out=dst, in_=src)
+                else:
+                    nc.scalar.copy(out=dst, in_=src)
 
         def quantise_weights(n):
             w_codes[n] = w_keep.tile([P, K_PASSES * GROUP_F], U32, align_bytes=64, name="w_codes")
@@ -174,7 +169,7 @@ def tile_dcadecoderblock_pa_kernel(
 
         def project(n, l):
             for i in range(GROUP):
-                ft = feature_tile(n, i)
+                ft = n * GROUP + i
                 acc = psum_acc.tile([P, TOK], F32, tag="acc")
                 for g in range(K_PASSES):
                     w_cols = slice(g * GROUP_F + i * P, g * GROUP_F + (i + 1) * P)
@@ -224,32 +219,33 @@ def tile_dcadecoderblock_pa_kernel(
             nc.vector.tensor_scalar_mul(out=neg_mean[:, rts], in0=mean_var[:, rts, 0], scalar1=-1.0)
             nc.vector.reciprocal(out=rstd[:, rts], in_=std[:, rts])
 
-        def normalised_parts(l, half):
-            for j in range(TOK_TILES):
-                rt = l * TOK_TILES + j
-                z_part[l, j, half] = norm_pool.tile([P, BANK], F32, name="z_part", tag="norm")
-                nc.gpsimd.tensor_scalar(
-                    out=z_part[l, j, half][:],
-                    in0=x_sb[:, rt, half * BANK : (half + 1) * BANK],
-                    scalar1=neg_mean[:, rt : rt + 1],
-                    scalar2=rstd[:, rt : rt + 1],
-                    op0=ALU.add,
-                    op1=ALU.mult,
-                )
+        def normalised_parts(l):
+            for half in range(DIM // BANK):
+                for j in range(TOK_TILES):
+                    rt = l * TOK_TILES + j
+                    z_part[l, j, half] = norm_pool.tile([P, BANK], F32, name="z_part", tag="norm")
+                    nc.gpsimd.tensor_scalar(
+                        out=z_part[l, j, half][:],
+                        in0=x_sb[:, rt, half * BANK : (half + 1) * BANK],
+                        scalar1=neg_mean[:, rt : rt + 1],
+                        scalar2=rstd[:, rt : rt + 1],
+                        op0=ALU.add,
+                        op1=ALU.mult,
+                    )
 
         def norm_terms(f):
             half, f_in_half = divmod(f, BANK // P)
             f_cols = slice(f_in_half * P, (f_in_half + 1) * P)
             zt = psum_tp.tile([P, BANK], F32, tag="tp")
             for j in range(TOK_TILES):
-                for l in reversed(range(LAYERS)):
+                for l in range(LAYERS):
                     nc.tensor.matmul(
                         out=zt[:, j * P : (j + 1) * P],
                         lhsT=z_part[l, j, half][:, f_cols],
                         rhs=ident_f32[:],
                         is_transpose=True,
-                        start=(l == LAYERS - 1),
-                        stop=(l == 0),
+                        start=(l == 0),
+                        stop=(l == LAYERS - 1),
                     )
             for t in range(PROJ):
                 ft = t * F_TILES + f
@@ -260,17 +256,17 @@ def tile_dcadecoderblock_pa_kernel(
                 )
 
         def finish_group(n):
-            half, t = divmod(n, PROJ)
+            t, half = divmod(n, 2)
             adder = nc.vector if n == GROUPS - 1 else nc.gpsimd
             for i in range(GROUP):
-                ft = feature_tile(n, i)
+                ft = n * GROUP + i
                 adder.tensor_tensor(out=ln_term[ft][:], in0=ln_term[ft][:], in1=relu_sum[ft][:], op=ALU.add)
             for j in range(TOK_TILES):
                 b, h = divmod(j, 2)
                 back = psum_tp.tile([P, BANK], F32, tag="tp")
                 for i in range(GROUP):
                     nc.tensor.transpose(
-                        back[:, i * P : (i + 1) * P], ln_term[feature_tile(n, i)][:, j * P : (j + 1) * P], ident_f32[:]
+                        back[:, i * P : (i + 1) * P], ln_term[n * GROUP + i][:, j * P : (j + 1) * P], ident_f32[:]
                     )
                 rows = rows_pool.tile([P, GROUP_F], F32)
                 nc.any.tensor_copy(out=rows[:], in_=back[:])
@@ -285,29 +281,25 @@ def tile_dcadecoderblock_pa_kernel(
         quantise_layer(1)
         project(0, 0)
         layer_statistics(0)
-        normalised_parts(0, 0)
+        normalised_parts(0)
         quantise_layer(2)
         project(0, 1)
         layer_statistics(1)
-        normalised_parts(1, 0)
+        normalised_parts(1)
         regroup_weights(1)
         quantise_weights(1)
         project(0, 2)
         layer_statistics(2)
-        normalised_parts(2, 0)
-        for l in range(LAYERS):
-            normalised_parts(l, 1)
+        normalised_parts(2)
+        for f in range(F_TILES):
+            norm_terms(f)
         for n in range(1, GROUPS):
             if n + 2 < GROUPS:
                 load_weights(n + 2)
             if n + 1 < GROUPS:
                 regroup_weights(n + 1)
                 quantise_weights(n + 1)
-            half_due, odd = divmod(n, 2)
             for l in range(LAYERS):
                 project(n, l)
-                if odd and half_due < HALVES and l < GROUP // 2:
-                    norm_terms(half_due * GROUP + 2 * l)
-                    norm_terms(half_due * GROUP + 2 * l + 1)
             finish_group(n - 1)
         finish_group(GROUPS - 1)

from contextlib import ExitStack

import concourse.mybir as mybir
from concourse.masks import make_identity

F32 = mybir.dt.float32
BF16 = mybir.dt.bfloat16
U32 = mybir.dt.uint32
U8 = mybir.dt.uint8
FP8X4 = mybir.dt.float8_e4m3fn_x4
ACT = mybir.ActivationFunctionType
ALU = mybir.AluOpType

P = 128
PACK = 4
K_PASS = P * PACK

BATCH, LAYERS, SEQ, DIM = 2, 3, 256, 1024
EPS = 1e-5
PROJ = 3
K_PASSES = DIM // K_PASS
TOK = BATCH * SEQ
TOK_TILES = TOK // P
F_TILES = DIM // P
GROUP = 4
GROUP_F = GROUP * P
GROUPS = PROJ * F_TILES // GROUP
BANK = 512
STATS = 6
STATS_MAX = 512

FLOPS = 2 * BATCH * LAYERS * SEQ * DIM * PROJ * DIM


def tile_dcadecoderblock_pa_kernel(
    tc,
    layer_outputs,
    grn_q_W, grn_q_b, grn_q_g, grn_q_be,
    grn_k_W, grn_k_b, grn_k_g, grn_k_be,
    grn_v_W, grn_v_b, grn_v_g, grn_v_be,
    out_0, out_1, out_2,
):
    nc = tc.nc
    weights = [grn_q_W, grn_k_W, grn_v_W]
    outs = [out_0, out_1, out_2]
    vectors = [grn_q_b, grn_k_b, grn_v_b, grn_q_g, grn_k_g, grn_v_g, grn_q_be, grn_k_be, grn_v_be]
    n_ft = PROJ * F_TILES

    with ExitStack() as ctx:
        const = ctx.enter_context(tc.tile_pool(name="const", bufs=1))
        x_stage = ctx.enter_context(tc.tile_pool(name="x_stage", bufs=2))
        w_load = ctx.enter_context(tc.tile_pool(name="w_load", bufs=3))
        w_stage = ctx.enter_context(tc.tile_pool(name="w_stage", bufs=2))
        w_keep = ctx.enter_context(tc.tile_pool(name="w_keep", bufs=3))
        norm_pool = ctx.enter_context(tc.tile_pool(name="norm", bufs=36))
        sums = ctx.enter_context(tc.tile_pool(name="sums", bufs=14))
        rows_pool = ctx.enter_context(tc.tile_pool(name="rows", bufs=4))
        psum_acc = ctx.enter_context(tc.psum_pool(name="psum_acc", bufs=5))
        psum_tp = ctx.enter_context(tc.psum_pool(name="psum_tp", bufs=3))

        ident_f32 = const.tile([P, P], F32)
        make_identity(nc, ident_f32[:])
        ident_bf16 = const.tile([P, P], BF16)
        make_identity(nc, ident_bf16[:])
        eps = const.tile([P, 1], F32)
        nc.vector.memset(eps[:], EPS)
        table_warm = const.tile([P, 1], F32)
        nc.scalar.activation(out=table_warm[:], in_=eps[:], func=ACT.Sqrt)

        x_sb = const.tile([P, LAYERS * TOK_TILES, DIM], BF16)

        def load_layer(l):
            for b in range(BATCH):
                rt = l * TOK_TILES + 2 * b
                nc.sync.dma_start(
                    out=x_sb[:, rt : rt + 2, :],
                    in_=layer_outputs[b, l, :, :].rearrange("(h p) d -> p h d", p=P),
                )

        w_raw = {}

        def load_weights(n):
            t, half = divmod(n, 2)
            w_raw[n] = w_load.tile([P, K_PASSES, PACK, GROUP_F], BF16, name="w_raw")
            for g in range(K_PASSES):
                for u in range(2):
                    k0 = g * K_PASS + u * 2 * P
                    nc.sync.dma_start(
                        out=w_raw[n][:, g, 2 * u : 2 * u + 2, :],
                        in_=weights[t][k0 : k0 + 2 * P, half * GROUP_F : (half + 1) * GROUP_F].rearrange(
                            "(p e) c -> p e c", e=2
                        ),
                    )

        vec_rows = const.tile([P, P], BF16)
        nc.vector.memset(vec_rows[:], 0.0)
        for v, vec in enumerate(vectors):
            nc.scalar.dma_start(
                out=vec_rows[v * F_TILES : (v + 1) * F_TILES, :],
                in_=vec.rearrange("(r c) -> r c", c=P),
            )

        load_layer(0)
        load_weights(0)
        load_layer(1)
        load_layer(2)
        load_weights(1)
        load_weights(2)

        x_codes = const.tile([P, LAYERS * K_PASSES * TOK], U32, align_bytes=64)
        x_scales = const.tile([P, LAYERS * K_PASSES * TOK], U8, align_bytes=64)

        def quantise_layer(l):
            grouped = x_stage.tile([P, K_PASSES * TOK * PACK], BF16, align_bytes=64)
            grouped_words = grouped[:].bitcast(F32).rearrange("p (g r u) -> p g r u", g=K_PASSES, u=2)
            for j in range(TOK_TILES):
                x_words = x_sb[:, l * TOK_TILES + j, :].bitcast(F32)
                xt = psum_tp.tile([P, BANK], F32, tag="tp")
                for gu in range(BANK // P):
                    nc.tensor.transpose(xt[:, gu * P : (gu + 1) * P], x_words[:, gu * P : (gu + 1) * P], ident_f32[:])
                nc.scalar.copy(
                    out=grouped_words[:, :, j * P : (j + 1) * P, :],
                    in_=xt[:].rearrange("p (g u r) -> p g r u", g=K_PASSES, u=2),
                )
            cols = slice(l * K_PASSES * TOK, (l + 1) * K_PASSES * TOK)
            nc.vector.quantize_mx(out=x_codes[:, cols].bitcast(FP8X4), scales=x_scales[:, cols], in_=grouped[:])

        w_grouped = {}
        w_codes = {}
        w_scales = {}

        def regroup_weights(n):
            w_grouped[n] = w_stage.tile([P, K_PASSES, GROUP_F, PACK], BF16, align_bytes=64, name="w_grouped")
            for g in range(K_PASSES):
                dst = w_grouped[n][:, g, :, :].rearrange("p (c i) t -> p c t i", i=4)
                src = w_raw[n][:, g, :, :].rearrange("p t (c i) -> p c t i", i=4)
                if g == 0:
                    nc.vector.tensor_copy(out=dst, in_=src)
                else:
                    nc.scalar.copy(out=dst, in_=src)

        def quantise_weights(n):
            w_codes[n] = w_keep.tile([P, K_PASSES * GROUP_F], U32, align_bytes=64, name="w_codes")
            w_scales[n] = w_keep.tile([P, K_PASSES * GROUP_F], U8, align_bytes=64, name="w_scales")
            nc.vector.quantize_mx(
                out=w_codes[n][:].bitcast(FP8X4),
                scales=w_scales[n][:],
                in_=w_grouped[n][:].rearrange("p g c t -> p (g c t)"),
            )

        params = const.tile([P, P], F32)
        neg_bias = const.tile([P, n_ft], F32)
        shift3 = const.tile([P, n_ft], F32)
        const_term = const.tile([P, n_ft], F32)

        def spread_vectors():
            vec_cols = psum_tp.tile([P, P], BF16, tag="tp")
            nc.tensor.transpose(vec_cols[:], vec_rows[:], ident_bf16[:])
            nc.vector.tensor_copy(out=params[:], in_=vec_cols[:])
            bias = params[:, 0:n_ft]
            shift = params[:, 2 * n_ft : 3 * n_ft]
            nc.vector.tensor_scalar_mul(out=neg_bias[:], in0=bias, scalar1=-1.0)
            nc.vector.tensor_scalar_mul(out=shift3[:], in0=shift, scalar1=float(LAYERS))
            nc.vector.scalar_tensor_tensor(
                out=const_term[:], in0=bias, scalar=float(LAYERS - 1), in1=shift3[:], op0=ALU.mult, op1=ALU.add
            )

        relu_sum = {}

        def project(n, l):
            for i in range(GROUP):
                ft = n * GROUP + i
                acc = psum_acc.tile([P, TOK], F32, tag="acc")
                for g in range(K_PASSES):
                    w_cols = slice(g * GROUP_F + i * P, g * GROUP_F + (i + 1) * P)
                    x_cols = slice((l * K_PASSES + g) * TOK, (l * K_PASSES + g + 1) * TOK)
                    nc.tensor.matmul_mx(
                        out=acc[:],
                        lhsT=w_codes[n][:, w_cols].bitcast(FP8X4),
                        lhsT_scale=w_scales[n][:, w_cols],
                        rhs=x_codes[:, x_cols].bitcast(FP8X4),
                        rhs_scale=x_scales[:, x_cols],
                        start=(g == 0),
                        stop=(g == K_PASSES - 1),
                    )
                if l == 0:
                    relu_sum[ft] = sums.tile([P, TOK], F32, name="relu_sum")
                    nc.scalar.activation(
                        out=relu_sum[ft][:], in_=acc[:], func=ACT.Relu, bias=params[:, ft : ft + 1], scale=1.0
                    )
                else:
                    nc.vector.scalar_tensor_tensor(
                        out=relu_sum[ft][:],
                        in0=acc[:],
                        scalar=neg_bias[:, ft : ft + 1],
                        in1=relu_sum[ft][:],
                        op0=ALU.max,
                        op1=ALU.add,
                    )

        n_rt = LAYERS * TOK_TILES
        chunks = DIM // STATS_MAX
        stats = const.tile([P, n_rt, chunks, STATS], F32)
        mean_var = const.tile([P, n_rt, 2], F32)
        std = const.tile([P, n_rt], F32)
        rstd = const.tile([P, n_rt], F32)
        neg_mean = const.tile([P, n_rt], F32)
        z_part = {}
        ln_term = {}

        def layer_statistics(l):
            for j in range(TOK_TILES):
                rt = l * TOK_TILES + j
                for c in range(chunks):
                    nc.vector.bn_stats(out=stats[:, rt, c, :], in_=x_sb[:, rt, c * STATS_MAX : (c + 1) * STATS_MAX])
                nc.vector.bn_aggr(out=mean_var[:, rt, :], in_=stats[:, rt, :, :].rearrange("p c s -> p (c s)"))
            rts = slice(l * TOK_TILES, (l + 1) * TOK_TILES)
            nc.scalar.activation(out=std[:, rts], in_=mean_var[:, rts, 1], func=ACT.Sqrt, bias=eps[:, 0:1], scale=1.0)
            nc.vector.tensor_scalar_mul(out=neg_mean[:, rts], in0=mean_var[:, rts, 0], scalar1=-1.0)
            nc.vector.reciprocal(out=rstd[:, rts], in_=std[:, rts])

        def normalised_parts(l):
            for half in range(DIM // BANK):
                for j in range(TOK_TILES):
                    rt = l * TOK_TILES + j
                    z_part[l, j, half] = norm_pool.tile([P, BANK], F32, name="z_part", tag="norm")
                    nc.gpsimd.tensor_scalar(
                        out=z_part[l, j, half][:],
                        in0=x_sb[:, rt, half * BANK : (half + 1) * BANK],
                        scalar1=neg_mean[:, rt : rt + 1],
                        scalar2=rstd[:, rt : rt + 1],
                        op0=ALU.add,
                        op1=ALU.mult,
                    )

        def norm_terms(f):
            half, f_in_half = divmod(f, BANK // P)
            f_cols = slice(f_in_half * P, (f_in_half + 1) * P)
            zt = psum_tp.tile([P, BANK], F32, tag="tp")
            for j in range(TOK_TILES):
                for l in range(LAYERS):
                    nc.tensor.matmul(
                        out=zt[:, j * P : (j + 1) * P],
                        lhsT=z_part[l, j, half][:, f_cols],
                        rhs=ident_f32[:],
                        is_transpose=True,
                        start=(l == 0),
                        stop=(l == LAYERS - 1),
                    )
            for t in range(PROJ):
                ft = t * F_TILES + f
                ln_term[ft] = norm_pool.tile([P, TOK], F32, name="ln_term", tag="norm")
                nc.scalar.activation(
                    out=ln_term[ft][:], in_=zt[:], func=ACT.Identity,
                    scale=params[:, n_ft + ft : n_ft + ft + 1], bias=const_term[:, ft : ft + 1],
                )

        def finish_group(n):
            t, half = divmod(n, 2)
            adder = nc.vector if n == GROUPS - 1 else nc.gpsimd
            for i in range(GROUP):
                ft = n * GROUP + i
                adder.tensor_tensor(out=ln_term[ft][:], in0=ln_term[ft][:], in1=relu_sum[ft][:], op=ALU.add)
            for j in range(TOK_TILES):
                b, h = divmod(j, 2)
                back = psum_tp.tile([P, BANK], F32, tag="tp")
                for i in range(GROUP):
                    nc.tensor.transpose(
                        back[:, i * P : (i + 1) * P], ln_term[n * GROUP + i][:, j * P : (j + 1) * P], ident_f32[:]
                    )
                rows = rows_pool.tile([P, GROUP_F], F32)
                nc.any.tensor_copy(out=rows[:], in_=back[:])
                nc.sync.dma_start(
                    out=outs[t][b, h * P : (h + 1) * P, half * GROUP_F : (half + 1) * GROUP_F], in_=rows[:]
                )

        quantise_layer(0)
        regroup_weights(0)
        quantise_weights(0)
        spread_vectors()
        quantise_layer(1)
        project(0, 0)
        layer_statistics(0)
        normalised_parts(0)
        quantise_layer(2)
        project(0, 1)
        layer_statistics(1)
        normalised_parts(1)
        regroup_weights(1)
        quantise_weights(1)
        project(0, 2)
        layer_statistics(2)
        normalised_parts(2)
        for f in range(F_TILES):
            norm_terms(f)
        for n in range(1, GROUPS):
            if n + 2 < GROUPS:
                load_weights(n + 2)
            if n + 1 < GROUPS:
                regroup_weights(n + 1)
                quantise_weights(n + 1)
            for l in range(LAYERS):
                project(n, l)
            finish_group(n - 1)
        finish_group(GROUPS - 1)
